import numpy as np
import ml_dtypes


def mxq(x, axis, fmt="e4m3"):
    dtype, down = {"e4m3": (ml_dtypes.float8_e4m3fn, 7), "e5m2": (ml_dtypes.float8_e5m2, 14)}[fmt]
    v = np.moveaxis(np.asarray(x, np.float32).astype(ml_dtypes.bfloat16).astype(np.float64), axis, -1)
    blocks = v.reshape(v.shape[:-1] + (-1, 32))
    amax = np.abs(blocks).max(-1, keepdims=True)
    byte = np.maximum(np.where(amax > 0, np.frexp(amax)[1] - 1 + 127, 0) - down, 1)
    scale = np.exp2(byte - 127.0)
    codes = (blocks / scale).astype(np.float32).astype(dtype).astype(np.float64)
    return np.moveaxis((codes * scale).reshape(v.shape), -1, axis)


WIDE = False


def mx_kscale(k):
    if not WIDE:
        return np.ones(k)
    levels = np.array([10, -10, 5, -5, 0])
    a = np.random.permutation(np.resize(levels, k // 512 * 4)).reshape(k // 512, 4)
    idx = np.arange(k)
    return np.exp2(a[idx // 512, idx % 128 // 32])


BF16 = ml_dtypes.bfloat16


def bf(x):
    return np.asarray(x, np.float32).astype(BF16)


def f64(x):
    return np.asarray(x).astype(np.float64)


B, S, F = 16, 512, 512


def stab(feature):
    var = np.var(feature, axis=2, ddof=1, keepdims=True)
    stability = 1.0 / (var + 1e-6)
    return stability / np.max(stability)


def setup_inputs():
    s = mx_kscale(S)
    s = s / s.min()
    r = np.exp2(np.random.uniform(-0.3, 0.3, (B, S, 1)))
    f0 = np.random.standard_normal((B, S, F)) * r * 2.0
    n0 = np.random.standard_normal((B, S, S)) * 3.0
    feature = bf(f0 * s[None, :, None])
    logits = n0 * stab(f64(bf(f0))) - np.log(s)[None, None, :]
    noise = bf(logits / stab(f64(feature)))
    return {"feature": feature, "noise": noise}


def reference(feature, noise):
    feature, noise = f64(feature), f64(noise)
    stability = stab(feature)
    scaled = noise * stability
    e = np.exp(scaled - scaled.max(-1, keepdims=True))
    return (mxq(e, 2, "e4m3") @ mxq(feature, 1, "e4m3")) / e.sum(-1, keepdims=True)

@@ -1,0 +1,241 @@
+from contextlib import ExitStack
+
+import concourse.mybir as mybir
+from concourse.masks import make_identity
+
+FLOPS = 2 * 16 * 512 * 512 * 512
+
+BF16 = mybir.dt.bfloat16
+F32 = mybir.dt.float32
+U32 = mybir.dt.uint32
+U8 = mybir.dt.uint8
+FP8X4 = mybir.dt.float8_e4m3fn_x4
+ALU = mybir.AluOpType
+ACT = mybir.ActivationFunctionType
+AX = mybir.AxisListType
+
+P = 128
+NB = 16
+T = 4
+W = 512
+
+
+def tile_frameaugment_t_kernel(tc, feature, noise, out):
+    nc = tc.nc
+    feat_v = feature.rearrange("b (p t) f -> b p t f", t=T)
+    noise_v = noise.rearrange("b (p t) j -> b p t j", t=T)
+    out_v = out.rearrange("b (p t) f -> b p t f", t=T)
+
+    s_var = [b for b in range(NB) if b % 3 == 1]
+    v_var = [b for b in range(NB) if b not in s_var]
+    col = dict((b, T * i) for i, b in enumerate(v_var + s_var))
+    nv = T * len(v_var)
+    ns = T * len(s_var)
+
+    with ExitStack() as ctx:
+        ctx.enter_context(tc.manual_schedule())
+        const = ctx.enter_context(tc.tile_pool(name="const", bufs=1))
+        raw = ctx.enter_context(tc.tile_pool(name="raw", bufs=20))
+        work = ctx.enter_context(tc.tile_pool(name="work", bufs=2))
+        psum_t = ctx.enter_context(tc.psum_pool(name="psum_t", bufs=2))
+        psum_o = ctx.enter_context(tc.psum_pool(name="psum_o", bufs=6))
+
+        ft = []
+        for b in range(NB):
+            x = raw.tile([P, T, W], BF16, name="ft%d" % b, tag="raw")
+            nc.sync.dma_start(out=x[:], in_=feat_v[b])
+            ft.append(x)
+        nt = []
+        for b in range(NB):
+            x = raw.tile([P, T, W], BF16, name="nt%d" % b, tag="raw")
+            nc.sync.dma_start(out=x[:], in_=noise_v[b])
+            nt.append(x)
+
+        warm = const.tile([P, 1], F32)
+        nc.vector.memset(warm[:], 0.0)
+        warm2 = const.tile([P, 1], F32)
+        nc.scalar.activation(out=warm2[:], in_=warm[:], func=ACT.Exp)
+        ident_b = const.tile([P, P], BF16)
+        make_identity(nc, ident_b[:])
+        ident_f = const.tile([P, P], F32)
+        make_identity(nc, ident_f[:])
+
+        st = const.tile([P, nv, 6], F32)
+        sx = const.tile([P, ns], F32)
+        nm = const.tile([P, ns], F32)
+        m2s = const.tile([P, ns], F32)
+        dd = const.tile([P, nv], F32)
+        mm = const.tile([P, nv], F32)
+        var = const.tile([P, T * NB], F32)
+        rv = const.tile([P, T * NB], F32)
+        sc = const.tile([P, T * NB], F32)
+        nmax = const.tile([P, T * NB], F32)
+        nbias = const.tile([P, T * NB], F32)
+        rsum = const.tile([P, T * NB], F32)
+        rrec = const.tile([P, T * NB], F32)
+        pmin = const.tile([P, 1], F32)
+        gmin = const.tile([P, 1], F32)
+        bc = const.tile([P, P], F32)
+        fc = const.tile([P, NB, W], U32, align_bytes=64)
+        fs = const.tile([P, NB, W], U8, align_bytes=64)
+
+        gfs = {}
+        es = {}
+        qs = {}
+
+        def variance(b):
+            c0 = col[b]
+            if b in s_var:
+                k0 = c0 - nv
+                for t in range(T):
+                    junk = work.tile([P, W], BF16, name="junk", tag="junk")
+                    nc.scalar.activation(out=junk[:], in_=ft[b][:, t, :], func=ACT.Copy,
+                                         accum_out=sx[:, k0 + t:k0 + t + 1])
+                nc.scalar.mul(out=nm[:, k0:k0 + T], in_=sx[:, k0:k0 + T], mul=-1.0 / W)
+                for t in range(T):
+                    junk = work.tile([P, W], BF16, name="junk", tag="junk")
+                    nc.scalar.activation(out=junk[:], in_=ft[b][:, t, :], func=ACT.Square,
+                                         bias=nm[:, k0 + t:k0 + t + 1],
+                                         accum_out=m2s[:, k0 + t:k0 + t + 1])
+            else:
+                for t in range(T):
+                    nc.vector.bn_stats(out=st[:, c0 + t, :], in_=ft[b][:, t, :])
+
+        def feat_regroup(b):
+            gf = work.tile([P, W, T], BF16, name="gf", tag="gf", align_bytes=64, bufs=13)
+            gfs[b] = gf
+            dst = gf[:].rearrange("p (c i) t -> p c t i", i=4)
+            src = ft[b][:].rearrange("p t (c i) -> p c t i", i=4)
+            if True:
+                nc.gpsimd.tensor_scalar(out=gf[:], in0=ft[b][:].rearrange("p t f -> p f t"), scalar1=1.0, scalar2=0.0,
+                                        op0=ALU.mult, op1=ALU.add)
+            else:
+                nc.vector.tensor_copy(out=dst, in_=src)
+
+        def feat_quant(b):
+            nc.vector.quantize_mx(out=fc[:, b, :].bitcast(FP8X4), scales=fs[:, b, :],
+                                  in_=gfs[b][:].rearrange("p f t -> p (f t)"))
+
+        def rowmax(b):
+            c0 = col[b]
+            f1 = work.tile([P, T, 256], BF16, name="f1", tag="f1", bufs=1)
+            nc.vector.tensor_tensor(out=f1[:], in0=nt[b][:, :, 0:256], in1=nt[b][:, :, 256:512], op=ALU.max)
+            f2 = work.tile([P, T, 128], BF16, name="f2", tag="f2", bufs=1)
+            nc.vector.tensor_tensor(out=f2[:], in0=f1[:, :, 0:128], in1=f1[:, :, 128:256], op=ALU.max)
+            f3 = work.tile([P, T, 64], BF16, name="f3", tag="f3", bufs=1)
+            nc.vector.tensor_tensor(out=f3[:], in0=f2[:, :, 0:64], in1=f2[:, :, 64:128], op=ALU.max)
+            f4 = work.tile([P, T, 32], BF16, name="f4", tag="f4", bufs=1)
+            nc.vector.tensor_tensor(out=f4[:], in0=f3[:, :, 0:32], in1=f3[:, :, 32:64], op=ALU.max)
+            nc.vector.tensor_reduce(out=nmax[:, c0:c0 + T], in_=f4[:], axis=AX.X, op=ALU.max)
+
+        def stabilities():
+            nc.vector.tensor_tensor(out=dd[:], in0=st[:, :, 1], in1=st[:, :, 4], op=ALU.subtract)
+            nc.vector.tensor_tensor(out=mm[:], in0=st[:, :, 2], in1=st[:, :, 5], op=ALU.add)
+            nc.vector.tensor_tensor(out=dd[:], in0=dd[:], in1=dd[:], op=ALU.mult)
+            nc.vector.scalar_tensor_tensor(out=mm[:], in0=dd[:], scalar=float(W // 4), in1=mm[:],
+                                           op0=ALU.mult, op1=ALU.add)
+            nc.vector.tensor_scalar(out=var[:, 0:nv], in0=mm[:], scalar1=1.0 / (W - 1), scalar2=1e-6,
+                                    op0=ALU.mult, op1=ALU.add)
+            nc.vector.tensor_scalar(out=var[:, nv:], in0=m2s[:], scalar1=1.0 / (W - 1), scalar2=1e-6,
+                                    op0=ALU.mult, op1=ALU.add)
+            nc.vector.tensor_reduce(out=pmin[:], in_=var[:], axis=AX.X, op=ALU.min)
+            nc.vector.tensor_copy(out=bc[:], in_=pmin[:].to_broadcast([P, P]))
+            pm = psum_o.tile([P, P], F32, name="pm", tag="po")
+            nc.tensor.transpose(pm[:], bc[:], ident_f[:])
+            nc.vector.reciprocal(out=rv[:], in_=var[:])
+            nc.vector.tensor_reduce(out=gmin[:], in_=pm[:], axis=AX.X, op=ALU.min)
+            nc.vector.tensor_scalar(out=sc[:], in0=rv[:], scalar1=gmin[:, 0:1], scalar2=None, op0=ALU.mult)
+
+        def bias(b):
+            c0 = col[b]
+            nc.vector.scalar_tensor_tensor(out=nbias[:, c0:c0 + T], in0=sc[:, c0:c0 + T], scalar=-1.0,
+                                           in1=nmax[:, c0:c0 + T], op0=ALU.mult, op1=ALU.mult)
+
+        def exps(b):
+            c0 = col[b]
+            e = work.tile([P, T, W], BF16, name="e", tag="e")
+            for t in range(T):
+                nc.scalar.activation(out=e[:, t, :], in_=nt[b][:, t, :], func=ACT.Exp,
+                                     bias=nbias[:, c0 + t:c0 + t + 1], scale=sc[:, c0 + t:c0 + t + 1],
+                                     accum_out=rsum[:, c0 + t:c0 + t + 1])
+            es[b] = e
+
+        def transposes(b):
+            e = es[b]
+            pts = []
+            for h in range(2):
+                pt = psum_t.tile([P, 2, T, P], BF16, name="pt", tag="pt")
+                for u in range(2):
+                    ev = e[:, 2 * h + u, :].rearrange("p (c k) -> p k c", k=T)
+                    for k in range(T):
+                        nc.tensor.transpose(pt[:, u, k, :], ev[:, k, :], ident_b[:])
+                pts.append(pt)
+            return pts
+
+        def regroup_e(b, pts):
+            g = work.tile([P, T, P, T], BF16, name="g", tag="g", align_bytes=64)
+            for h in range(2):
+                nc.vector.tensor_copy(out=g[:, 2 * h:2 * h + 2, :, :],
+                                      in_=pts[h][:].rearrange("p u k i -> p u i k"))
+            return g
+
+        def quant_e(b, g):
+            ec = work.tile([P, W], U32, name="ec", tag="ec", align_bytes=64)
+            esc = work.tile([P, W], U8, name="esc", tag="esc", align_bytes=64)
+            nc.vector.quantize_mx(out=ec[:].bitcast(FP8X4), scales=esc[:],
+                                  in_=g[:].rearrange("p u i k -> p (u i k)"))
+            c0 = col[b]
+            nc.vector.reciprocal(out=rrec[:, c0:c0 + T], in_=rsum[:, c0:c0 + T])
+            qs[b] = (ec, esc)
+
+        def products(b):
+            ec, esc = qs[b]
+            pos = []
+            for t in range(T):
+                po = psum_o.tile([P, W], F32, name="po", tag="po")
+                nc.tensor.matmul_mx(out=po[:], lhsT=ec[:, P * t:P * t + P].bitcast(FP8X4),
+                                    lhsT_scale=esc[:, P * t:P * t + P],
+                                    rhs=fc[:, b, :].bitcast(FP8X4), rhs_scale=fs[:, b, :],
+                                    start=True, stop=True)
+                pos.append(po)
+            return pos
+
+        def finish(b, pos):
+            c0 = col[b]
+            last = b == NB - 1
+            o = work.tile([P, T, W], F32, name="o", tag="o", bufs=3)
+            for t in range(T):
+                if last and t % 2 == 1:
+                    nc.vector.tensor_scalar(out=o[:, t, :], in0=pos[t][:], scalar1=rrec[:, c0 + t:c0 + t + 1],
+                                            scalar2=None, op0=ALU.mult)
+                else:
+                    nc.scalar.activation(out=o[:, t, :], in_=pos[t][:], func=ACT.Copy,
+                                         scale=rrec[:, c0 + t:c0 + t + 1])
+                if last and t % 2 == 1:
+                    nc.sync.dma_start(out=out_v[b][:, t - 1:t + 1, :], in_=o[:, t - 1:t + 1, :])
+            if not last:
+                nc.sync.dma_start(out=out_v[b], in_=o[:])
+
+        for b in range(NB):
+            variance(b)
+            feat_regroup(b)
+        rowmax(0)
+        feat_quant(0)
+        stabilities()
+        bias(0)
+        pos = None
+        for i in range(NB + 1):
+            if i + 1 < NB:
+                rowmax(i + 1)
+                bias(i + 1)
+            if i >= 1:
+                pos = products(i - 1)
+            if i < NB:
+                exps(i)
+                pts = transposes(i)
+                g = regroup_e(i, pts)
+                if i + 1 < NB:
+                    feat_quant(i + 1)
+                quant_e(i, g)
+            if i >= 1:
+                finish(i - 1, pos)

@@ -22,9 +22,9 @@ W = 512
 
 def tile_frameaugment_t_kernel(tc, feature, noise, out):
     nc = tc.nc
-    feat_v = feature.rearrange("b (p t) f -> b p t f", t=T)
-    noise_v = noise.rearrange("b (p t) j -> b p t j", t=T)
-    out_v = out.rearrange("b (p t) f -> b p t f", t=T)
+    feat_v = feature.rearrange("b (t p) f -> b p t f", p=P)
+    noise_v = noise.rearrange("b (t p) j -> b p t j", p=P)
+    out_v = out.rearrange("b (t p) f -> b p t f", p=P)
 
     s_var = [b for b in range(NB) if b % 3 == 1]
     v_var = [b for b in range(NB) if b not in s_var]
@@ -37,8 +37,8 @@ def tile_frameaugment_t_kernel(tc, feature, noise, out):
         const = ctx.enter_context(tc.tile_pool(name="const", bufs=1))
         raw = ctx.enter_context(tc.tile_pool(name="raw", bufs=20))
         work = ctx.enter_context(tc.tile_pool(name="work", bufs=2))
-        psum_t = ctx.enter_context(tc.psum_pool(name="psum_t", bufs=2))
-        psum_o = ctx.enter_context(tc.psum_pool(name="psum_o", bufs=6))
+        psum_t = ctx.enter_context(tc.psum_pool(name="psum_t", bufs=4))
+        psum_o = ctx.enter_context(tc.psum_pool(name="psum_o", bufs=4))
 
         ft = []
         for b in range(NB):
@@ -166,9 +166,8 @@ def tile_frameaugment_t_kernel(tc, feature, noise, out):
             for h in range(2):
                 pt = psum_t.tile([P, 2, T, P], BF16, name="pt", tag="pt")
                 for u in range(2):
-                    ev = e[:, 2 * h + u, :].rearrange("p (c k) -> p k c", k=T)
                     for k in range(T):
-                        nc.tensor.transpose(pt[:, u, k, :], ev[:, k, :], ident_b[:])
+                        nc.tensor.transpose(pt[:, u, k, :], e[:, 2 * h + u, P * k:P * k + P], ident_b[:])
                 pts.append(pt)
             return pts
 
@@ -220,22 +219,24 @@ def tile_frameaugment_t_kernel(tc, feature, noise, out):
             variance(b)
             feat_regroup(b)
         rowmax(0)
-        feat_quant(0)
         stabilities()
         bias(0)
-        pos = None
-        for i in range(NB + 1):
-            if i + 1 < NB:
-                rowmax(i + 1)
-                bias(i + 1)
+        pts = {}
+        for i in range(-2, NB + 1):
+            if i + 2 < NB:
+                exps(i + 2)
             if i >= 1:
                 pos = products(i - 1)
-            if i < NB:
-                exps(i)
-                pts = transposes(i)
-                g = regroup_e(i, pts)
-                if i + 1 < NB:
-                    feat_quant(i + 1)
+            if 0 <= i + 1 < NB:
+                pts[i + 1] = transposes(i + 1)
+            if 0 <= i < NB:
+                g = regroup_e(i, pts[i])
+            if i + 3 < NB:
+                rowmax(i + 3)
+                bias(i + 3)
+            if 0 <= i + 1 < NB:
+                feat_quant(i + 1)
+            if 0 <= i < NB:
                 quant_e(i, g)
             if i >= 1:
                 finish(i - 1, pos)

@@ -33,7 +33,7 @@ def tile_frameaugment_t_kernel(tc, feature, noise, out):
     ns = T * len(s_var)
 
     with ExitStack() as ctx:
-        ctx.enter_context(tc.manual_schedule())
+        pass
         const = ctx.enter_context(tc.tile_pool(name="const", bufs=1))
         raw = ctx.enter_context(tc.tile_pool(name="raw", bufs=20))
         work = ctx.enter_context(tc.tile_pool(name="work", bufs=2))
@@ -69,15 +69,15 @@ def tile_frameaugment_t_kernel(tc, feature, noise, out):
         var = const.tile([P, T * NB], F32)
         rv = const.tile([P, T * NB], F32)
         sc = const.tile([P, T * NB], F32)
-        nmax = const.tile([P, T * NB], F32)
-        nbias = const.tile([P, T * NB], F32)
-        rsum = const.tile([P, T * NB], F32)
-        rrec = const.tile([P, T * NB], F32)
+        nmax = [const.tile([P, T], F32, name="nmax%d" % b) for b in range(NB)]
+        nbias = [const.tile([P, T], F32, name="nbias%d" % b) for b in range(NB)]
+        rsum = [const.tile([P, T], F32, name="rsum%d" % b) for b in range(NB)]
+        rrec = [const.tile([P, T], F32, name="rrec%d" % b) for b in range(NB)]
         pmin = const.tile([P, 1], F32)
         gmin = const.tile([P, 1], F32)
         bc = const.tile([P, P], F32)
-        fc = const.tile([P, NB, W], U32, align_bytes=64)
-        fs = const.tile([P, NB, W], U8, align_bytes=64)
+        fc = [const.tile([P, W], U32, name="fc%d" % b, align_bytes=64) for b in range(NB)]
+        fs = [const.tile([P, W], U8, name="fs%d" % b, align_bytes=64) for b in range(NB)]
 
         gfs = {}
         es = {}
@@ -113,7 +113,7 @@ def tile_frameaugment_t_kernel(tc, feature, noise, out):
                 nc.vector.tensor_copy(out=dst, in_=src)
 
         def feat_quant(b):
-            nc.vector.quantize_mx(out=fc[:, b, :].bitcast(FP8X4), scales=fs[:, b, :],
+            nc.vector.quantize_mx(out=fc[b][:].bitcast(FP8X4), scales=fs[b][:],
                                   in_=gfs[b][:].rearrange("p f t -> p (f t)"))
 
         def rowmax(b):
@@ -126,7 +126,7 @@ def tile_frameaugment_t_kernel(tc, feature, noise, out):
             nc.vector.tensor_tensor(out=f3[:], in0=f2[:, :, 0:64], in1=f2[:, :, 64:128], op=ALU.max)
             f4 = work.tile([P, T, 32], BF16, name="f4", tag="f4", bufs=1)
             nc.vector.tensor_tensor(out=f4[:], in0=f3[:, :, 0:32], in1=f3[:, :, 32:64], op=ALU.max)
-            nc.vector.tensor_reduce(out=nmax[:, c0:c0 + T], in_=f4[:], axis=AX.X, op=ALU.max)
+            nc.vector.tensor_reduce(out=nmax[b][:], in_=f4[:], axis=AX.X, op=ALU.max)
 
         def stabilities():
             nc.vector.tensor_tensor(out=dd[:], in0=st[:, :, 1], in1=st[:, :, 4], op=ALU.subtract)
@@ -148,16 +148,16 @@ def tile_frameaugment_t_kernel(tc, feature, noise, out):
 
         def bias(b):
             c0 = col[b]
-            nc.vector.scalar_tensor_tensor(out=nbias[:, c0:c0 + T], in0=sc[:, c0:c0 + T], scalar=-1.0,
-                                           in1=nmax[:, c0:c0 + T], op0=ALU.mult, op1=ALU.mult)
+            nc.vector.scalar_tensor_tensor(out=nbias[b][:], in0=sc[:, c0:c0 + T], scalar=-1.0,
+                                           in1=nmax[b][:], op0=ALU.mult, op1=ALU.mult)
 
         def exps(b):
             c0 = col[b]
             e = work.tile([P, T, W], BF16, name="e", tag="e")
             for t in range(T):
                 nc.scalar.activation(out=e[:, t, :], in_=nt[b][:, t, :], func=ACT.Exp,
-                                     bias=nbias[:, c0 + t:c0 + t + 1], scale=sc[:, c0 + t:c0 + t + 1],
-                                     accum_out=rsum[:, c0 + t:c0 + t + 1])
+                                     bias=nbias[b][:, t:t + 1], scale=sc[:, c0 + t:c0 + t + 1],
+                                     accum_out=rsum[b][:, t:t + 1])
             es[b] = e
 
         def transposes(b):
@@ -184,7 +184,7 @@ def tile_frameaugment_t_kernel(tc, feature, noise, out):
             nc.vector.quantize_mx(out=ec[:].bitcast(FP8X4), scales=esc[:],
                                   in_=g[:].rearrange("p u i k -> p (u i k)"))
             c0 = col[b]
-            nc.vector.reciprocal(out=rrec[:, c0:c0 + T], in_=rsum[:, c0:c0 + T])
+            nc.vector.reciprocal(out=rrec[b][:], in_=rsum[b][:])
             qs[b] = (ec, esc)
 
         def products(b):
@@ -194,7 +194,7 @@ def tile_frameaugment_t_kernel(tc, feature, noise, out):
                 po = psum_o.tile([P, W], F32, name="po", tag="po")
                 nc.tensor.matmul_mx(out=po[:], lhsT=ec[:, P * t:P * t + P].bitcast(FP8X4),
                                     lhsT_scale=esc[:, P * t:P * t + P],
-                                    rhs=fc[:, b, :].bitcast(FP8X4), rhs_scale=fs[:, b, :],
+                                    rhs=fc[b][:].bitcast(FP8X4), rhs_scale=fs[b][:],
                                     start=True, stop=True)
                 pos.append(po)
             return pos
@@ -205,11 +205,11 @@ def tile_frameaugment_t_kernel(tc, feature, noise, out):
             o = work.tile([P, T, W], F32, name="o", tag="o", bufs=3)
             for t in range(T):
                 if last and t % 2 == 1:
-                    nc.vector.tensor_scalar(out=o[:, t, :], in0=pos[t][:], scalar1=rrec[:, c0 + t:c0 + t + 1],
+                    nc.vector.tensor_scalar(out=o[:, t, :], in0=pos[t][:], scalar1=rrec[b][:, t:t + 1],
                                             scalar2=None, op0=ALU.mult)
                 else:
                     nc.scalar.activation(out=o[:, t, :], in_=pos[t][:], func=ACT.Copy,
-                                         scale=rrec[:, c0 + t:c0 + t + 1])
+                                         scale=rrec[b][:, t:t + 1])
                 if last and t % 2 == 1:
                     nc.sync.dma_start(out=out_v[b][:, t - 1:t + 1, :], in_=o[:, t - 1:t + 1, :])
             if not last:

@@ -18,6 +18,14 @@ P = 128
 NB = 16
 T = 4
 W = 512
+EPS = 1e-6
+
+
+def weave(first, second):
+    for n in range(max(len(first), len(second))):
+        for steps in (first, second):
+            if n < len(steps):
+                steps[n]()
 
 
 def tile_frameaugment_t_kernel(tc, feature, noise, out):
@@ -27,13 +35,13 @@ def tile_frameaugment_t_kernel(tc, feature, noise, out):
     out_v = out.rearrange("b (t p) f -> b p t f", p=P)
 
     s_var = [b for b in range(NB) if b % 3 == 1]
-    v_var = [b for b in range(NB) if b not in s_var]
-    col = dict((b, T * i) for i, b in enumerate(v_var + s_var))
+    v_var = [b for b in range(NB) if b % 3 != 1]
+    col = dict((b, T * n) for n, b in enumerate(v_var + s_var))
     nv = T * len(v_var)
     ns = T * len(s_var)
 
     with ExitStack() as ctx:
-        pass
+        ctx.enter_context(tc.manual_schedule())
         const = ctx.enter_context(tc.tile_pool(name="const", bufs=1))
         raw = ctx.enter_context(tc.tile_pool(name="raw", bufs=20))
         work = ctx.enter_context(tc.tile_pool(name="work", bufs=2))
@@ -43,7 +51,11 @@ def tile_frameaugment_t_kernel(tc, feature, noise, out):
         ft = []
         for b in range(NB):
             x = raw.tile([P, T, W], BF16, name="ft%d" % b, tag="raw")
-            nc.sync.dma_start(out=x[:], in_=feat_v[b])
+            if b < 2:
+                for t in range(T):
+                    nc.sync.dma_start(out=x[:, t, :], in_=feat_v[b][:, t, :])
+            else:
+                nc.sync.dma_start(out=x[:], in_=feat_v[b])
             ft.append(x)
         nt = []
         for b in range(NB):
@@ -65,86 +77,67 @@ def tile_frameaugment_t_kernel(tc, feature, noise, out):
         nm = const.tile([P, ns], F32)
         m2s = const.tile([P, ns], F32)
         dd = const.tile([P, nv], F32)
+        d2 = const.tile([P, nv], F32)
         mm = const.tile([P, nv], F32)
         var = const.tile([P, T * NB], F32)
         rv = const.tile([P, T * NB], F32)
         sc = const.tile([P, T * NB], F32)
+        pmin = const.tile([P, 1], F32)
+        gmin = const.tile([P, 1], F32)
+        bc = const.tile([P, P], F32)
         nmax = [const.tile([P, T], F32, name="nmax%d" % b) for b in range(NB)]
         nbias = [const.tile([P, T], F32, name="nbias%d" % b) for b in range(NB)]
         rsum = [const.tile([P, T], F32, name="rsum%d" % b) for b in range(NB)]
         rrec = [const.tile([P, T], F32, name="rrec%d" % b) for b in range(NB)]
-        pmin = const.tile([P, 1], F32)
-        gmin = const.tile([P, 1], F32)
-        bc = const.tile([P, P], F32)
         fc = [const.tile([P, W], U32, name="fc%d" % b, align_bytes=64) for b in range(NB)]
         fs = [const.tile([P, W], U8, name="fs%d" % b, align_bytes=64) for b in range(NB)]
 
         gfs = {}
         es = {}
+        pts = {}
+        gs = {}
         qs = {}
+        pos = {}
 
-        def variance(b):
-            c0 = col[b]
-            if b in s_var:
-                k0 = c0 - nv
-                for t in range(T):
-                    junk = work.tile([P, W], BF16, name="junk", tag="junk")
-                    nc.scalar.activation(out=junk[:], in_=ft[b][:, t, :], func=ACT.Copy,
-                                         accum_out=sx[:, k0 + t:k0 + t + 1])
-                nc.scalar.mul(out=nm[:, k0:k0 + T], in_=sx[:, k0:k0 + T], mul=-1.0 / W)
-                for t in range(T):
-                    junk = work.tile([P, W], BF16, name="junk", tag="junk")
-                    nc.scalar.activation(out=junk[:], in_=ft[b][:, t, :], func=ACT.Square,
-                                         bias=nm[:, k0 + t:k0 + t + 1],
-                                         accum_out=m2s[:, k0 + t:k0 + t + 1])
-            else:
-                for t in range(T):
-                    nc.vector.bn_stats(out=st[:, c0 + t, :], in_=ft[b][:, t, :])
+        def scalar_variance(b):
+            k0 = col[b] - nv
+            for t in range(T):
+                junk = work.tile([P, W], BF16, name="junk", tag="junk")
+                nc.scalar.activation(out=junk[:], in_=ft[b][:, t, :], func=ACT.Copy,
+                                     accum_out=sx[:, k0 + t:k0 + t + 1])
+            nc.scalar.mul(out=nm[:, k0:k0 + T], in_=sx[:, k0:k0 + T], mul=-1.0 / W)
+            for t in range(T):
+                junk = work.tile([P, W], BF16, name="junk", tag="junk")
+                nc.scalar.activation(out=junk[:], in_=ft[b][:, t, :], func=ACT.Square,
+                                     bias=nm[:, k0 + t:k0 + t + 1],
+                                     accum_out=m2s[:, k0 + t:k0 + t + 1])
+
+        def stats_step(b, t):
+            return lambda: nc.vector.bn_stats(out=st[:, col[b] + t, :], in_=ft[b][:, t, :])
 
         def feat_regroup(b):
             gf = work.tile([P, W, T], BF16, name="gf", tag="gf", align_bytes=64, bufs=13)
             gfs[b] = gf
-            dst = gf[:].rearrange("p (c i) t -> p c t i", i=4)
-            src = ft[b][:].rearrange("p t (c i) -> p c t i", i=4)
-            if True:
-                nc.gpsimd.tensor_scalar(out=gf[:], in0=ft[b][:].rearrange("p t f -> p f t"), scalar1=1.0, scalar2=0.0,
-                                        op0=ALU.mult, op1=ALU.add)
-            else:
-                nc.vector.tensor_copy(out=dst, in_=src)
+            nc.gpsimd.tensor_scalar(out=gf[:], in0=ft[b][:].rearrange("p t f -> p f t"), scalar1=1.0, scalar2=0.0,
+                                    op0=ALU.mult, op1=ALU.add)
 
         def feat_quant(b):
             nc.vector.quantize_mx(out=fc[b][:].bitcast(FP8X4), scales=fs[b][:],
                                   in_=gfs[b][:].rearrange("p f t -> p (f t)"))
 
-        def rowmax(b):
-            c0 = col[b]
-            f1 = work.tile([P, T, 256], BF16, name="f1", tag="f1", bufs=1)
-            nc.vector.tensor_tensor(out=f1[:], in0=nt[b][:, :, 0:256], in1=nt[b][:, :, 256:512], op=ALU.max)
-            f2 = work.tile([P, T, 128], BF16, name="f2", tag="f2", bufs=1)
-            nc.vector.tensor_tensor(out=f2[:], in0=f1[:, :, 0:128], in1=f1[:, :, 128:256], op=ALU.max)
-            f3 = work.tile([P, T, 64], BF16, name="f3", tag="f3", bufs=1)
-            nc.vector.tensor_tensor(out=f3[:], in0=f2[:, :, 0:64], in1=f2[:, :, 64:128], op=ALU.max)
-            f4 = work.tile([P, T, 32], BF16, name="f4", tag="f4", bufs=1)
-            nc.vector.tensor_tensor(out=f4[:], in0=f3[:, :, 0:32], in1=f3[:, :, 32:64], op=ALU.max)
-            nc.vector.tensor_reduce(out=nmax[b][:], in_=f4[:], axis=AX.X, op=ALU.max)
+        def rowmax_steps(b):
+            widths = (256, 128, 64, 32)
+            halves = [work.tile([P, T, w], BF16, name="half%d" % w, tag="half%d" % w) for w in widths]
+            sources = [nt[b]] + halves[:-1]
 
-        def stabilities():
-            nc.vector.tensor_tensor(out=dd[:], in0=st[:, :, 1], in1=st[:, :, 4], op=ALU.subtract)
-            nc.vector.tensor_tensor(out=mm[:], in0=st[:, :, 2], in1=st[:, :, 5], op=ALU.add)
-            nc.vector.tensor_tensor(out=dd[:], in0=dd[:], in1=dd[:], op=ALU.mult)
-            nc.vector.scalar_tensor_tensor(out=mm[:], in0=dd[:], scalar=float(W // 4), in1=mm[:],
-                                           op0=ALU.mult, op1=ALU.add)
-            nc.vector.tensor_scalar(out=var[:, 0:nv], in0=mm[:], scalar1=1.0 / (W - 1), scalar2=1e-6,
-                                    op0=ALU.mult, op1=ALU.add)
-            nc.vector.tensor_scalar(out=var[:, nv:], in0=m2s[:], scalar1=1.0 / (W - 1), scalar2=1e-6,
-                                    op0=ALU.mult, op1=ALU.add)
-            nc.vector.tensor_reduce(out=pmin[:], in_=var[:], axis=AX.X, op=ALU.min)
-            nc.vector.tensor_copy(out=bc[:], in_=pmin[:].to_broadcast([P, P]))
-            pm = psum_o.tile([P, P], F32, name="pm", tag="po")
-            nc.tensor.transpose(pm[:], bc[:], ident_f[:])
-            nc.vector.reciprocal(out=rv[:], in_=var[:])
-            nc.vector.tensor_reduce(out=gmin[:], in_=pm[:], axis=AX.X, op=ALU.min)
-            nc.vector.tensor_scalar(out=sc[:], in0=rv[:], scalar1=gmin[:, 0:1], scalar2=None, op0=ALU.mult)
+            def halving(n):
+                w = widths[n]
+                return lambda: nc.vector.tensor_tensor(out=halves[n][:], in0=sources[n][:, :, 0:w],
+                                                       in1=sources[n][:, :, w:2 * w], op=ALU.max)
+
+            steps = [halving(n) for n in range(len(widths))]
+            steps.append(lambda: nc.vector.tensor_reduce(out=nmax[b][:], in_=halves[-1][:], axis=AX.X, op=ALU.max))
+            return steps
 
         def bias(b):
             c0 = col[b]
@@ -162,81 +155,107 @@ def tile_frameaugment_t_kernel(tc, feature, noise, out):
 
         def transposes(b):
             e = es[b]
-            pts = []
+            pts[b] = []
             for h in range(2):
                 pt = psum_t.tile([P, 2, T, P], BF16, name="pt", tag="pt")
                 for u in range(2):
                     for k in range(T):
                         nc.tensor.transpose(pt[:, u, k, :], e[:, 2 * h + u, P * k:P * k + P], ident_b[:])
-                pts.append(pt)
-            return pts
+                pts[b].append(pt)
 
-        def regroup_e(b, pts):
-            g = work.tile([P, T, P, T], BF16, name="g", tag="g", align_bytes=64)
-            for h in range(2):
-                nc.vector.tensor_copy(out=g[:, 2 * h:2 * h + 2, :, :],
-                                      in_=pts[h][:].rearrange("p u k i -> p u i k"))
-            return g
+        def regroup_step(b, h):
+            def step():
+                if h == 0:
+                    gs[b] = work.tile([P, T, P, T], BF16, name="g", tag="g", align_bytes=64)
+                nc.vector.tensor_copy(out=gs[b][:, 2 * h:2 * h + 2, :, :],
+                                      in_=pts[b][h][:].rearrange("p u k i -> p u i k"))
+            return step
 
-        def quant_e(b, g):
+        def quant_e(b):
             ec = work.tile([P, W], U32, name="ec", tag="ec", align_bytes=64)
             esc = work.tile([P, W], U8, name="esc", tag="esc", align_bytes=64)
             nc.vector.quantize_mx(out=ec[:].bitcast(FP8X4), scales=esc[:],
-                                  in_=g[:].rearrange("p u i k -> p (u i k)"))
-            c0 = col[b]
-            nc.vector.reciprocal(out=rrec[b][:], in_=rsum[b][:])
+                                  in_=gs[b][:].rearrange("p u i k -> p (u i k)"))
             qs[b] = (ec, esc)
+
+        def recip(b):
+            nc.vector.reciprocal(out=rrec[b][:], in_=rsum[b][:])
 
         def products(b):
             ec, esc = qs[b]
-            pos = []
+            pos[b] = []
             for t in range(T):
                 po = psum_o.tile([P, W], F32, name="po", tag="po")
                 nc.tensor.matmul_mx(out=po[:], lhsT=ec[:, P * t:P * t + P].bitcast(FP8X4),
                                     lhsT_scale=esc[:, P * t:P * t + P],
                                     rhs=fc[b][:].bitcast(FP8X4), rhs_scale=fs[b][:],
                                     start=True, stop=True)
-                pos.append(po)
-            return pos
+                pos[b].append(po)
 
-        def finish(b, pos):
-            c0 = col[b]
+        def finish(b):
             last = b == NB - 1
             o = work.tile([P, T, W], F32, name="o", tag="o", bufs=3)
             for t in range(T):
                 if last and t % 2 == 1:
-                    nc.vector.tensor_scalar(out=o[:, t, :], in0=pos[t][:], scalar1=rrec[b][:, t:t + 1],
+                    nc.vector.tensor_scalar(out=o[:, t, :], in0=pos[b][t][:], scalar1=rrec[b][:, t:t + 1],
                                             scalar2=None, op0=ALU.mult)
-                else:
-                    nc.scalar.activation(out=o[:, t, :], in_=pos[t][:], func=ACT.Copy,
-                                         scale=rrec[b][:, t:t + 1])
-                if last and t % 2 == 1:
                     nc.sync.dma_start(out=out_v[b][:, t - 1:t + 1, :], in_=o[:, t - 1:t + 1, :])
+                else:
+                    nc.scalar.activation(out=o[:, t, :], in_=pos[b][t][:], func=ACT.Copy,
+                                         scale=rrec[b][:, t:t + 1])
             if not last:
                 nc.sync.dma_start(out=out_v[b], in_=o[:])
 
         for b in range(NB):
-            variance(b)
+            if b in s_var:
+                scalar_variance(b)
             feat_regroup(b)
-        rowmax(0)
-        stabilities()
-        bias(0)
-        pts = {}
+        stats = [stats_step(b, t) for b in v_var for t in range(T)]
+        first_max = rowmax_steps(0)
+        for step in stats[:-len(first_max)]:
+            step()
+        weave(stats[-len(first_max):], first_max)
+
+        pm = psum_o.tile([P, P], F32, name="pm", tag="po")
+        chain = [
+            lambda: nc.vector.tensor_tensor(out=dd[:], in0=st[:, :, 1], in1=st[:, :, 4], op=ALU.subtract),
+            lambda: nc.vector.scalar_tensor_tensor(out=mm[:], in0=st[:, :, 2], scalar=EPS * (W - 1), in1=st[:, :, 5],
+                                                   op0=ALU.add, op1=ALU.add),
+            lambda: nc.vector.scalar_tensor_tensor(out=d2[:], in0=dd[:], scalar=float(W // 4), in1=dd[:],
+                                                   op0=ALU.mult, op1=ALU.mult),
+            lambda: nc.vector.tensor_scalar(out=var[:, nv:], in0=m2s[:], scalar1=EPS * (W - 1), scalar2=None,
+                                            op0=ALU.add),
+            lambda: nc.vector.tensor_tensor(out=var[:, 0:nv], in0=d2[:], in1=mm[:], op=ALU.add),
+            lambda: nc.vector.tensor_reduce(out=pmin[:], in_=var[:], axis=AX.X, op=ALU.min),
+            lambda: nc.tensor.transpose(pm[:], pmin[:].to_broadcast([P, P]), ident_f[:]),
+            lambda: nc.vector.reciprocal(out=rv[:], in_=var[:]),
+            lambda: nc.vector.tensor_reduce(out=gmin[:], in_=pm[:], axis=AX.X, op=ALU.min),
+            lambda: nc.vector.tensor_scalar(out=sc[:], in0=rv[:], scalar1=gmin[:, 0:1], scalar2=None, op0=ALU.mult),
+            lambda: bias(0),
+        ]
+        weave(chain, rowmax_steps(1) + rowmax_steps(2))
+        bias(1)
+        bias(2)
+
         for i in range(-2, NB + 1):
             if i + 2 < NB:
                 exps(i + 2)
             if i >= 1:
-                pos = products(i - 1)
+                products(i - 1)
             if 0 <= i + 1 < NB:
-                pts[i + 1] = transposes(i + 1)
+                transposes(i + 1)
+            folds = rowmax_steps(i + 3) if 3 <= i + 3 < NB else []
+            others = []
             if 0 <= i < NB:
-                g = regroup_e(i, pts[i])
-            if i + 3 < NB:
-                rowmax(i + 3)
+                others.append(regroup_step(i, 0))
+                others.append(regroup_step(i, 1))
+            if 0 <= i + 1 < NB:
+                others.append(lambda: feat_quant(i + 1))
+            if 0 <= i < NB:
+                others.append(lambda: quant_e(i))
+                others.append(lambda: recip(i))
+            weave(folds, others)
+            if folds:
                 bias(i + 3)
-            if 0 <= i + 1 < NB:
-                feat_quant(i + 1)
-            if 0 <= i < NB:
-                quant_e(i, g)
             if i >= 1:
-                finish(i - 1, pos)
+                finish(i - 1)

@@ -19,6 +19,8 @@ NB = 16
 T = 4
 W = 512
 EPS = 1e-6
+G_LAST = 9
+S_LAST = 11
 
 
 def weave(first, second):
@@ -43,7 +45,7 @@ def tile_frameaugment_t_kernel(tc, feature, noise, out):
     with ExitStack() as ctx:
         ctx.enter_context(tc.manual_schedule())
         const = ctx.enter_context(tc.tile_pool(name="const", bufs=1))
-        raw = ctx.enter_context(tc.tile_pool(name="raw", bufs=20))
+        raw = ctx.enter_context(tc.tile_pool(name="raw", bufs=21))
         work = ctx.enter_context(tc.tile_pool(name="work", bufs=2))
         psum_t = ctx.enter_context(tc.psum_pool(name="psum_t", bufs=4))
         psum_o = ctx.enter_context(tc.psum_pool(name="psum_o", bufs=4))
@@ -116,10 +118,17 @@ def tile_frameaugment_t_kernel(tc, feature, noise, out):
             return lambda: nc.vector.bn_stats(out=st[:, col[b] + t, :], in_=ft[b][:, t, :])
 
         def feat_regroup(b):
-            gf = work.tile([P, W, T], BF16, name="gf", tag="gf", align_bytes=64, bufs=13)
+            gf = work.tile([P, W, T], BF16, name="gf", tag="gf", align_bytes=64, bufs=12)
             gfs[b] = gf
-            nc.gpsimd.tensor_scalar(out=gf[:], in0=ft[b][:].rearrange("p t f -> p f t"), scalar1=1.0, scalar2=0.0,
-                                    op0=ALU.mult, op1=ALU.add)
+            by_fours = gf[:].rearrange("p (c i) t -> p c t i", i=4)
+            fours = ft[b][:].rearrange("p t (c i) -> p c t i", i=4)
+            if b < G_LAST:
+                nc.gpsimd.tensor_scalar(out=gf[:], in0=ft[b][:].rearrange("p t f -> p f t"), scalar1=1.0,
+                                        scalar2=0.0, op0=ALU.mult, op1=ALU.add)
+            elif b < S_LAST:
+                nc.scalar.copy(out=by_fours, in_=fours)
+            else:
+                nc.vector.tensor_copy(out=by_fours, in_=fours)
 
         def feat_quant(b):
             nc.vector.quantize_mx(out=fc[b][:].bitcast(FP8X4), scales=fs[b][:],
@@ -209,12 +218,11 @@ def tile_frameaugment_t_kernel(tc, feature, noise, out):
         for b in range(NB):
             if b in s_var:
                 scalar_variance(b)
+        for b in range(S_LAST):
             feat_regroup(b)
-        stats = [stats_step(b, t) for b in v_var for t in range(T)]
-        first_max = rowmax_steps(0)
-        for step in stats[:-len(first_max)]:
-            step()
-        weave(stats[-len(first_max):], first_max)
+        for b in v_var:
+            for t in range(T):
+                stats_step(b, t)()
 
         pm = psum_o.tile([P, P], F32, name="pm", tag="po")
         chain = [
@@ -233,9 +241,8 @@ def tile_frameaugment_t_kernel(tc, feature, noise, out):
             lambda: nc.vector.tensor_scalar(out=sc[:], in0=rv[:], scalar1=gmin[:, 0:1], scalar2=None, op0=ALU.mult),
             lambda: bias(0),
         ]
-        weave(chain, rowmax_steps(1) + rowmax_steps(2))
+        weave(chain, rowmax_steps(0) + rowmax_steps(1))
         bias(1)
-        bias(2)
 
         for i in range(-2, NB + 1):
             if i + 2 < NB:
@@ -244,13 +251,15 @@ def tile_frameaugment_t_kernel(tc, feature, noise, out):
                 products(i - 1)
             if 0 <= i + 1 < NB:
                 transposes(i + 1)
-            folds = rowmax_steps(i + 3) if 3 <= i + 3 < NB else []
+            folds = rowmax_steps(i + 3) if 2 <= i + 3 < NB else []
             others = []
             if 0 <= i < NB:
                 others.append(regroup_step(i, 0))
                 others.append(regroup_step(i, 1))
             if 0 <= i + 1 < NB:
                 others.append(lambda: feat_quant(i + 1))
+            if S_LAST <= i + 3 < NB:
+                others.append(lambda: feat_regroup(i + 3))
             if 0 <= i < NB:
                 others.append(lambda: quant_e(i))
                 others.append(lambda: recip(i))

@@ -180,12 +180,14 @@ def tile_frameaugment_t_kernel(tc, feature, noise, out):
                                       in_=pts[b][h][:].rearrange("p u k i -> p u i k"))
             return step
 
-        def quant_e(b):
-            ec = work.tile([P, W], U32, name="ec", tag="ec", align_bytes=64)
-            esc = work.tile([P, W], U8, name="esc", tag="esc", align_bytes=64)
-            nc.vector.quantize_mx(out=ec[:].bitcast(FP8X4), scales=esc[:],
-                                  in_=gs[b][:].rearrange("p u i k -> p (u i k)"))
-            qs[b] = (ec, esc)
+        def quant_e(b, h):
+            if h == 0:
+                qs[b] = (work.tile([P, W], U32, name="ec", tag="ec", align_bytes=64),
+                         work.tile([P, W], U8, name="esc", tag="esc", align_bytes=64))
+            ec, esc = qs[b]
+            cols = slice(2 * P * h, 2 * P * (h + 1))
+            nc.vector.quantize_mx(out=ec[:, cols].bitcast(FP8X4), scales=esc[:, cols],
+                                  in_=gs[b][:, 2 * h:2 * h + 2, :, :].rearrange("p u i k -> p (u i k)"))
 
         def recip(b):
             nc.vector.reciprocal(out=rrec[b][:], in_=rsum[b][:])
@@ -241,16 +243,16 @@ def tile_frameaugment_t_kernel(tc, feature, noise, out):
             lambda: nc.vector.tensor_scalar(out=sc[:], in0=rv[:], scalar1=gmin[:, 0:1], scalar2=None, op0=ALU.mult),
             lambda: bias(0),
         ]
-        weave(chain, rowmax_steps(0) + rowmax_steps(1))
+        weave(chain, [step for pair in zip(rowmax_steps(0), rowmax_steps(1)) for step in pair])
         bias(1)
 
         for i in range(-2, NB + 1):
             if i + 2 < NB:
                 exps(i + 2)
-            if i >= 1:
-                products(i - 1)
             if 0 <= i + 1 < NB:
                 transposes(i + 1)
+            if i >= 1:
+                products(i - 1)
             folds = rowmax_steps(i + 3) if 2 <= i + 3 < NB else []
             others = []
             if 0 <= i < NB:
@@ -261,7 +263,8 @@ def tile_frameaugment_t_kernel(tc, feature, noise, out):
             if S_LAST <= i + 3 < NB:
                 others.append(lambda: feat_regroup(i + 3))
             if 0 <= i < NB:
-                others.append(lambda: quant_e(i))
+                others.append(lambda: quant_e(i, 0))
+                others.append(lambda: quant_e(i, 1))
                 others.append(lambda: recip(i))
             weave(folds, others)
             if folds:

@@ -43,7 +43,7 @@ def tile_frameaugment_t_kernel(tc, feature, noise, out):
     ns = T * len(s_var)
 
     with ExitStack() as ctx:
-        ctx.enter_context(tc.manual_schedule())
+        pass
         const = ctx.enter_context(tc.tile_pool(name="const", bufs=1))
         raw = ctx.enter_context(tc.tile_pool(name="raw", bufs=21))
         work = ctx.enter_context(tc.tile_pool(name="work", bufs=2))

@@ -15,12 +15,15 @@ ACT = mybir.ActivationFunctionType
 AX = mybir.AxisListType
 
 P = 128
-NB = 16
-T = 4
+SEQS = 16
+Q = 4
 W = 512
 EPS = 1e-6
-G_LAST = 9
-S_LAST = 11
+STATS = 6
+
+SCALAR_VARIANCE_EVERY = 4
+GPSIMD_REGROUPS = 10
+SCALAR_REGROUPS = 15
 
 
 def weave(first, second):
@@ -32,242 +35,235 @@ def weave(first, second):
 
 def tile_frameaugment_t_kernel(tc, feature, noise, out):
     nc = tc.nc
-    feat_v = feature.rearrange("b (t p) f -> b p t f", p=P)
-    noise_v = noise.rearrange("b (t p) j -> b p t j", p=P)
-    out_v = out.rearrange("b (t p) f -> b p t f", p=P)
+    feature_quarters = feature.rearrange("b (t p) f -> b p t f", p=P)
+    noise_quarters = noise.rearrange("b (t p) j -> b p t j", p=P)
+    out_quarters = out.rearrange("b (t p) f -> b p t f", p=P)
 
-    s_var = [b for b in range(NB) if b % 3 == 1]
-    v_var = [b for b in range(NB) if b % 3 != 1]
-    col = dict((b, T * n) for n, b in enumerate(v_var + s_var))
-    nv = T * len(v_var)
-    ns = T * len(s_var)
+    scalar_seqs = [b for b in range(SEQS) if b % SCALAR_VARIANCE_EVERY == 1]
+    vector_seqs = [b for b in range(SEQS) if b % SCALAR_VARIANCE_EVERY != 1]
+    col = dict((b, Q * n) for n, b in enumerate(vector_seqs + scalar_seqs))
+    n_vector = Q * len(vector_seqs)
+    n_scalar = Q * len(scalar_seqs)
 
     with ExitStack() as ctx:
-        pass
-        const = ctx.enter_context(tc.tile_pool(name="const", bufs=1))
-        raw = ctx.enter_context(tc.tile_pool(name="raw", bufs=21))
+        ctx.enter_context(tc.manual_schedule())
+        keep = ctx.enter_context(tc.tile_pool(name="keep", bufs=1))
+        inputs = ctx.enter_context(tc.tile_pool(name="inputs", bufs=SEQS + SEQS - SCALAR_REGROUPS))
         work = ctx.enter_context(tc.tile_pool(name="work", bufs=2))
-        psum_t = ctx.enter_context(tc.psum_pool(name="psum_t", bufs=4))
-        psum_o = ctx.enter_context(tc.psum_pool(name="psum_o", bufs=4))
+        transposed_banks = ctx.enter_context(tc.psum_pool(name="transposed_banks", bufs=4))
+        product_banks = ctx.enter_context(tc.psum_pool(name="product_banks", bufs=Q))
 
-        ft = []
-        for b in range(NB):
-            x = raw.tile([P, T, W], BF16, name="ft%d" % b, tag="raw")
+        feature_in = []
+        for b in range(SEQS):
+            tile_in = inputs.tile([P, Q, W], BF16, name="feature_in%d" % b, tag="inputs")
             if b < 2:
-                for t in range(T):
-                    nc.sync.dma_start(out=x[:, t, :], in_=feat_v[b][:, t, :])
+                for t in range(Q):
+                    nc.sync.dma_start(out=tile_in[:, t, :], in_=feature_quarters[b][:, t, :])
             else:
-                nc.sync.dma_start(out=x[:], in_=feat_v[b])
-            ft.append(x)
-        nt = []
-        for b in range(NB):
-            x = raw.tile([P, T, W], BF16, name="nt%d" % b, tag="raw")
-            nc.sync.dma_start(out=x[:], in_=noise_v[b])
-            nt.append(x)
+                nc.sync.dma_start(out=tile_in[:], in_=feature_quarters[b])
+            feature_in.append(tile_in)
+        noise_in = []
+        for b in range(SEQS):
+            tile_in = inputs.tile([P, Q, W], BF16, name="noise_in%d" % b, tag="inputs")
+            nc.sync.dma_start(out=tile_in[:], in_=noise_quarters[b])
+            noise_in.append(tile_in)
 
-        warm = const.tile([P, 1], F32)
-        nc.vector.memset(warm[:], 0.0)
-        warm2 = const.tile([P, 1], F32)
-        nc.scalar.activation(out=warm2[:], in_=warm[:], func=ACT.Exp)
-        ident_b = const.tile([P, P], BF16)
-        make_identity(nc, ident_b[:])
-        ident_f = const.tile([P, P], F32)
-        make_identity(nc, ident_f[:])
+        zero = keep.tile([P, 1], F32)
+        nc.vector.memset(zero[:], 0.0)
+        one = keep.tile([P, 1], F32)
+        nc.scalar.activation(out=one[:], in_=zero[:], func=ACT.Exp)
+        identity_bf16 = keep.tile([P, P], BF16)
+        make_identity(nc, identity_bf16[:])
+        identity_f32 = keep.tile([P, P], F32)
+        make_identity(nc, identity_f32[:])
 
-        st = const.tile([P, nv, 6], F32)
-        sx = const.tile([P, ns], F32)
-        nm = const.tile([P, ns], F32)
-        m2s = const.tile([P, ns], F32)
-        dd = const.tile([P, nv], F32)
-        d2 = const.tile([P, nv], F32)
-        mm = const.tile([P, nv], F32)
-        var = const.tile([P, T * NB], F32)
-        rv = const.tile([P, T * NB], F32)
-        sc = const.tile([P, T * NB], F32)
-        pmin = const.tile([P, 1], F32)
-        gmin = const.tile([P, 1], F32)
-        bc = const.tile([P, P], F32)
-        nmax = [const.tile([P, T], F32, name="nmax%d" % b) for b in range(NB)]
-        nbias = [const.tile([P, T], F32, name="nbias%d" % b) for b in range(NB)]
-        rsum = [const.tile([P, T], F32, name="rsum%d" % b) for b in range(NB)]
-        rrec = [const.tile([P, T], F32, name="rrec%d" % b) for b in range(NB)]
-        fc = [const.tile([P, W], U32, name="fc%d" % b, align_bytes=64) for b in range(NB)]
-        fs = [const.tile([P, W], U8, name="fs%d" % b, align_bytes=64) for b in range(NB)]
+        stats = keep.tile([P, n_vector, STATS], F32)
+        sums = keep.tile([P, n_scalar], F32)
+        neg_means = keep.tile([P, n_scalar], F32)
+        scalar_m2 = keep.tile([P, n_scalar], F32)
+        mean_gap = keep.tile([P, n_vector], F32)
+        gap_term = keep.tile([P, n_vector], F32)
+        m2_even_odd = keep.tile([P, n_vector], F32)
+        spread = keep.tile([P, SEQS * Q], F32)
+        inv_spread = keep.tile([P, SEQS * Q], F32)
+        stability = keep.tile([P, SEQS * Q], F32)
+        partition_min = keep.tile([P, 1], F32)
+        global_min = keep.tile([P, 1], F32)
+        row_max = [keep.tile([P, Q], F32, name="row_max%d" % b) for b in range(SEQS)]
+        exp_bias = [keep.tile([P, Q], F32, name="exp_bias%d" % b) for b in range(SEQS)]
+        row_sum = [keep.tile([P, Q], F32, name="row_sum%d" % b) for b in range(SEQS)]
+        inv_row_sum = [keep.tile([P, Q], F32, name="inv_row_sum%d" % b) for b in range(SEQS)]
+        feature_codes = [keep.tile([P, W], U32, name="feature_codes%d" % b, align_bytes=64) for b in range(SEQS)]
+        feature_scales = [keep.tile([P, W], U8, name="feature_scales%d" % b, align_bytes=64) for b in range(SEQS)]
 
-        gfs = {}
-        es = {}
-        pts = {}
-        gs = {}
-        qs = {}
-        pos = {}
+        feature_grouped = {}
+        e_rows = {}
+        e_transposed = {}
+        e_grouped = {}
+        e_quantised = {}
+        products = {}
+
 
         def scalar_variance(b):
-            k0 = col[b] - nv
-            for t in range(T):
-                junk = work.tile([P, W], BF16, name="junk", tag="junk")
-                nc.scalar.activation(out=junk[:], in_=ft[b][:, t, :], func=ACT.Copy,
-                                     accum_out=sx[:, k0 + t:k0 + t + 1])
-            nc.scalar.mul(out=nm[:, k0:k0 + T], in_=sx[:, k0:k0 + T], mul=-1.0 / W)
-            for t in range(T):
-                junk = work.tile([P, W], BF16, name="junk", tag="junk")
-                nc.scalar.activation(out=junk[:], in_=ft[b][:, t, :], func=ACT.Square,
-                                     bias=nm[:, k0 + t:k0 + t + 1],
-                                     accum_out=m2s[:, k0 + t:k0 + t + 1])
+            first = col[b] - n_vector
+            for t in range(Q):
+                unused = work.tile([P, W], BF16, name="unused", tag="unused")
+                nc.scalar.activation(out=unused[:], in_=feature_in[b][:, t, :], func=ACT.Copy,
+                                     accum_out=sums[:, first + t:first + t + 1])
+            nc.scalar.mul(out=neg_means[:, first:first + Q], in_=sums[:, first:first + Q], mul=-1.0 / W)
+            for t in range(Q):
+                unused = work.tile([P, W], BF16, name="unused", tag="unused")
+                nc.scalar.activation(out=unused[:], in_=feature_in[b][:, t, :], func=ACT.Square,
+                                     bias=neg_means[:, first + t:first + t + 1],
+                                     accum_out=scalar_m2[:, first + t:first + t + 1])
 
-        def stats_step(b, t):
-            return lambda: nc.vector.bn_stats(out=st[:, col[b] + t, :], in_=ft[b][:, t, :])
-
-        def feat_regroup(b):
-            gf = work.tile([P, W, T], BF16, name="gf", tag="gf", align_bytes=64, bufs=12)
-            gfs[b] = gf
-            by_fours = gf[:].rearrange("p (c i) t -> p c t i", i=4)
-            fours = ft[b][:].rearrange("p t (c i) -> p c t i", i=4)
-            if b < G_LAST:
-                nc.gpsimd.tensor_scalar(out=gf[:], in0=ft[b][:].rearrange("p t f -> p f t"), scalar1=1.0,
-                                        scalar2=0.0, op0=ALU.mult, op1=ALU.add)
-            elif b < S_LAST:
-                nc.scalar.copy(out=by_fours, in_=fours)
+        def regroup_feature(b):
+            grouped = work.tile([P, W, Q], BF16, name="feature_grouped", tag="feature_grouped", align_bytes=64,
+                                bufs=SCALAR_REGROUPS + 1)
+            feature_grouped[b] = grouped
+            grouped_by_fours = grouped[:].rearrange("p (c i) t -> p c t i", i=4)
+            in_by_fours = feature_in[b][:].rearrange("p t (c i) -> p c t i", i=4)
+            if b < GPSIMD_REGROUPS:
+                nc.gpsimd.tensor_scalar(out=grouped[:], in0=feature_in[b][:].rearrange("p t f -> p f t"),
+                                        scalar1=1.0, scalar2=0.0, op0=ALU.mult, op1=ALU.add)
+            elif b < SCALAR_REGROUPS:
+                nc.scalar.copy(out=grouped_by_fours, in_=in_by_fours)
             else:
-                nc.vector.tensor_copy(out=by_fours, in_=fours)
+                nc.vector.tensor_copy(out=grouped_by_fours, in_=in_by_fours)
 
-        def feat_quant(b):
-            nc.vector.quantize_mx(out=fc[b][:].bitcast(FP8X4), scales=fs[b][:],
-                                  in_=gfs[b][:].rearrange("p f t -> p (f t)"))
+        def quantise_feature(b):
+            nc.vector.quantize_mx(out=feature_codes[b][:].bitcast(FP8X4), scales=feature_scales[b][:],
+                                  in_=feature_grouped[b][:].rearrange("p f t -> p (f t)"))
 
-        def rowmax_steps(b):
-            widths = (256, 128, 64, 32)
-            halves = [work.tile([P, T, w], BF16, name="half%d" % w, tag="half%d" % w) for w in widths]
-            sources = [nt[b]] + halves[:-1]
+        def row_max_steps(b):
+            widths = (W // 2, W // 4, W // 8, W // 16)
+            folded = [work.tile([P, Q, w], BF16, name="folded%d" % w, tag="folded%d" % w) for w in widths]
+            sources = [noise_in[b]] + folded[:-1]
 
-            def halving(n):
+            def fold(n):
                 w = widths[n]
-                return lambda: nc.vector.tensor_tensor(out=halves[n][:], in0=sources[n][:, :, 0:w],
+                return lambda: nc.vector.tensor_tensor(out=folded[n][:], in0=sources[n][:, :, 0:w],
                                                        in1=sources[n][:, :, w:2 * w], op=ALU.max)
 
-            steps = [halving(n) for n in range(len(widths))]
-            steps.append(lambda: nc.vector.tensor_reduce(out=nmax[b][:], in_=halves[-1][:], axis=AX.X, op=ALU.max))
+            steps = [fold(n) for n in range(len(widths))]
+            steps.append(lambda: nc.vector.tensor_reduce(out=row_max[b][:], in_=folded[-1][:], axis=AX.X, op=ALU.max))
             return steps
 
-        def bias(b):
-            c0 = col[b]
-            nc.vector.scalar_tensor_tensor(out=nbias[b][:], in0=sc[:, c0:c0 + T], scalar=-1.0,
-                                           in1=nmax[b][:], op0=ALU.mult, op1=ALU.mult)
+        def bias_of_exp(b):
+            nc.vector.scalar_tensor_tensor(out=exp_bias[b][:], in0=stability[:, col[b]:col[b] + Q], scalar=-1.0,
+                                           in1=row_max[b][:], op0=ALU.mult, op1=ALU.mult)
 
-        def exps(b):
-            c0 = col[b]
-            e = work.tile([P, T, W], BF16, name="e", tag="e")
-            for t in range(T):
-                nc.scalar.activation(out=e[:, t, :], in_=nt[b][:, t, :], func=ACT.Exp,
-                                     bias=nbias[b][:, t:t + 1], scale=sc[:, c0 + t:c0 + t + 1],
-                                     accum_out=rsum[b][:, t:t + 1])
-            es[b] = e
+        def exponentials(b):
+            e_rows[b] = work.tile([P, Q, W], BF16, name="e_rows", tag="e_rows")
+            for t in range(Q):
+                nc.scalar.activation(out=e_rows[b][:, t, :], in_=noise_in[b][:, t, :], func=ACT.Exp,
+                                     bias=exp_bias[b][:, t:t + 1], scale=stability[:, col[b] + t:col[b] + t + 1],
+                                     accum_out=row_sum[b][:, t:t + 1])
 
         def transposes(b):
-            e = es[b]
-            pts[b] = []
-            for h in range(2):
-                pt = psum_t.tile([P, 2, T, P], BF16, name="pt", tag="pt")
+            e_transposed[b] = []
+            for half in range(2):
+                bank = transposed_banks.tile([P, 2, Q, P], BF16, name="e_transposed", tag="e_transposed")
                 for u in range(2):
-                    for k in range(T):
-                        nc.tensor.transpose(pt[:, u, k, :], e[:, 2 * h + u, P * k:P * k + P], ident_b[:])
-                pts[b].append(pt)
+                    for k in range(Q):
+                        nc.tensor.transpose(bank[:, u, k, :], e_rows[b][:, 2 * half + u, P * k:P * k + P],
+                                            identity_bf16[:])
+                e_transposed[b].append(bank)
 
-        def regroup_step(b, h):
-            def step():
-                if h == 0:
-                    gs[b] = work.tile([P, T, P, T], BF16, name="g", tag="g", align_bytes=64)
-                nc.vector.tensor_copy(out=gs[b][:, 2 * h:2 * h + 2, :, :],
-                                      in_=pts[b][h][:].rearrange("p u k i -> p u i k"))
-            return step
+        def regroup_e(b, half):
+            if half == 0:
+                e_grouped[b] = work.tile([P, Q, P, Q], BF16, name="e_grouped", tag="e_grouped", align_bytes=64)
+            nc.vector.tensor_copy(out=e_grouped[b][:, 2 * half:2 * half + 2, :, :],
+                                  in_=e_transposed[b][half][:].rearrange("p u k i -> p u i k"))
 
-        def quant_e(b, h):
-            if h == 0:
-                qs[b] = (work.tile([P, W], U32, name="ec", tag="ec", align_bytes=64),
-                         work.tile([P, W], U8, name="esc", tag="esc", align_bytes=64))
-            ec, esc = qs[b]
-            cols = slice(2 * P * h, 2 * P * (h + 1))
-            nc.vector.quantize_mx(out=ec[:, cols].bitcast(FP8X4), scales=esc[:, cols],
-                                  in_=gs[b][:, 2 * h:2 * h + 2, :, :].rearrange("p u i k -> p (u i k)"))
+        def quantise_e(b, half):
+            if half == 0:
+                e_quantised[b] = (work.tile([P, W], U32, name="e_codes", tag="e_codes", align_bytes=64),
+                                  work.tile([P, W], U8, name="e_scales", tag="e_scales", align_bytes=64))
+            codes, scales = e_quantised[b]
+            cols = slice(2 * P * half, 2 * P * (half + 1))
+            nc.vector.quantize_mx(out=codes[:, cols].bitcast(FP8X4), scales=scales[:, cols],
+                                  in_=e_grouped[b][:, 2 * half:2 * half + 2, :, :].rearrange("p u i k -> p (u i k)"))
 
-        def recip(b):
-            nc.vector.reciprocal(out=rrec[b][:], in_=rsum[b][:])
+        def invert_row_sums(b):
+            nc.vector.reciprocal(out=inv_row_sum[b][:], in_=row_sum[b][:])
 
-        def products(b):
-            ec, esc = qs[b]
-            pos[b] = []
-            for t in range(T):
-                po = psum_o.tile([P, W], F32, name="po", tag="po")
-                nc.tensor.matmul_mx(out=po[:], lhsT=ec[:, P * t:P * t + P].bitcast(FP8X4),
-                                    lhsT_scale=esc[:, P * t:P * t + P],
-                                    rhs=fc[b][:].bitcast(FP8X4), rhs_scale=fs[b][:],
+        def multiply(b):
+            codes, scales = e_quantised[b]
+            products[b] = []
+            for t in range(Q):
+                bank = product_banks.tile([P, W], F32, name="product", tag="product")
+                nc.tensor.matmul_mx(out=bank[:], lhsT=codes[:, P * t:P * t + P].bitcast(FP8X4),
+                                    lhsT_scale=scales[:, P * t:P * t + P],
+                                    rhs=feature_codes[b][:].bitcast(FP8X4), rhs_scale=feature_scales[b][:],
                                     start=True, stop=True)
-                pos[b].append(po)
+                products[b].append(bank)
 
-        def finish(b):
-            last = b == NB - 1
-            o = work.tile([P, T, W], F32, name="o", tag="o", bufs=3)
-            for t in range(T):
+        def divide_and_store(b):
+            last = b == SEQS - 1
+            result = work.tile([P, Q, W], F32, name="result", tag="result", bufs=3)
+            for t in range(Q):
                 if last and t % 2 == 1:
-                    nc.vector.tensor_scalar(out=o[:, t, :], in0=pos[b][t][:], scalar1=rrec[b][:, t:t + 1],
-                                            scalar2=None, op0=ALU.mult)
-                    nc.sync.dma_start(out=out_v[b][:, t - 1:t + 1, :], in_=o[:, t - 1:t + 1, :])
+                    nc.vector.tensor_scalar(out=result[:, t, :], in0=products[b][t][:],
+                                            scalar1=inv_row_sum[b][:, t:t + 1], scalar2=None, op0=ALU.mult)
+                    nc.sync.dma_start(out=out_quarters[b][:, t - 1:t + 1, :], in_=result[:, t - 1:t + 1, :])
                 else:
-                    nc.scalar.activation(out=o[:, t, :], in_=pos[b][t][:], func=ACT.Copy,
-                                         scale=rrec[b][:, t:t + 1])
+                    nc.scalar.activation(out=result[:, t, :], in_=products[b][t][:], func=ACT.Copy,
+                                         scale=inv_row_sum[b][:, t:t + 1])
             if not last:
-                nc.sync.dma_start(out=out_v[b], in_=o[:])
+                nc.sync.dma_start(out=out_quarters[b], in_=result[:])
 
-        for b in range(NB):
-            if b in s_var:
-                scalar_variance(b)
-        for b in range(S_LAST):
-            feat_regroup(b)
-        for b in v_var:
-            for t in range(T):
-                stats_step(b, t)()
+        for b in scalar_seqs:
+            scalar_variance(b)
+        for b in range(SCALAR_REGROUPS):
+            regroup_feature(b)
+        for b in vector_seqs:
+            for t in range(Q):
+                nc.vector.bn_stats(out=stats[:, col[b] + t, :], in_=feature_in[b][:, t, :])
 
-        pm = psum_o.tile([P, P], F32, name="pm", tag="po")
+        all_minima = product_banks.tile([P, P], F32, name="all_minima", tag="product")
         chain = [
-            lambda: nc.vector.tensor_tensor(out=dd[:], in0=st[:, :, 1], in1=st[:, :, 4], op=ALU.subtract),
-            lambda: nc.vector.scalar_tensor_tensor(out=mm[:], in0=st[:, :, 2], scalar=EPS * (W - 1), in1=st[:, :, 5],
-                                                   op0=ALU.add, op1=ALU.add),
-            lambda: nc.vector.scalar_tensor_tensor(out=d2[:], in0=dd[:], scalar=float(W // 4), in1=dd[:],
-                                                   op0=ALU.mult, op1=ALU.mult),
-            lambda: nc.vector.tensor_scalar(out=var[:, nv:], in0=m2s[:], scalar1=EPS * (W - 1), scalar2=None,
-                                            op0=ALU.add),
-            lambda: nc.vector.tensor_tensor(out=var[:, 0:nv], in0=d2[:], in1=mm[:], op=ALU.add),
-            lambda: nc.vector.tensor_reduce(out=pmin[:], in_=var[:], axis=AX.X, op=ALU.min),
-            lambda: nc.tensor.transpose(pm[:], pmin[:].to_broadcast([P, P]), ident_f[:]),
-            lambda: nc.vector.reciprocal(out=rv[:], in_=var[:]),
-            lambda: nc.vector.tensor_reduce(out=gmin[:], in_=pm[:], axis=AX.X, op=ALU.min),
-            lambda: nc.vector.tensor_scalar(out=sc[:], in0=rv[:], scalar1=gmin[:, 0:1], scalar2=None, op0=ALU.mult),
-            lambda: bias(0),
+            lambda: nc.vector.tensor_tensor(out=mean_gap[:], in0=stats[:, :, 1], in1=stats[:, :, 4], op=ALU.subtract),
+            lambda: nc.vector.scalar_tensor_tensor(out=m2_even_odd[:], in0=stats[:, :, 2], scalar=EPS * (W - 1),
+                                                   in1=stats[:, :, 5], op0=ALU.add, op1=ALU.add),
+            lambda: nc.vector.scalar_tensor_tensor(out=gap_term[:], in0=mean_gap[:], scalar=float(W // 4),
+                                                   in1=mean_gap[:], op0=ALU.mult, op1=ALU.mult),
+            lambda: nc.vector.tensor_scalar(out=spread[:, n_vector:], in0=scalar_m2[:], scalar1=EPS * (W - 1),
+                                            scalar2=None, op0=ALU.add),
+            lambda: nc.vector.tensor_tensor(out=spread[:, 0:n_vector], in0=gap_term[:], in1=m2_even_odd[:], op=ALU.add),
+            lambda: nc.vector.tensor_reduce(out=partition_min[:], in_=spread[:], axis=AX.X, op=ALU.min),
+            lambda: nc.tensor.transpose(all_minima[:], partition_min[:].to_broadcast([P, P]), identity_f32[:]),
+            lambda: nc.vector.reciprocal(out=inv_spread[:], in_=spread[:]),
+            lambda: nc.vector.tensor_reduce(out=global_min[:], in_=all_minima[:], axis=AX.X, op=ALU.min),
+            lambda: nc.vector.tensor_scalar(out=stability[:], in0=inv_spread[:], scalar1=global_min[:, 0:1],
+                                            scalar2=None, op0=ALU.mult),
+            lambda: bias_of_exp(0),
         ]
-        weave(chain, [step for pair in zip(rowmax_steps(0), rowmax_steps(1)) for step in pair])
-        bias(1)
+        weave(chain, [step for pair in zip(row_max_steps(0), row_max_steps(1)) for step in pair])
+        bias_of_exp(1)
 
-        for i in range(-2, NB + 1):
-            if i + 2 < NB:
-                exps(i + 2)
-            if 0 <= i + 1 < NB:
+        for i in range(-2, SEQS + 1):
+            if i + 2 < SEQS:
+                exponentials(i + 2)
+            if 0 <= i + 1 < SEQS:
                 transposes(i + 1)
             if i >= 1:
-                products(i - 1)
-            folds = rowmax_steps(i + 3) if 2 <= i + 3 < NB else []
+                multiply(i - 1)
+            maxima = row_max_steps(i + 3) if 2 <= i + 3 < SEQS else []
             others = []
-            if 0 <= i < NB:
-                others.append(regroup_step(i, 0))
-                others.append(regroup_step(i, 1))
-            if 0 <= i + 1 < NB:
-                others.append(lambda: feat_quant(i + 1))
-            if S_LAST <= i + 3 < NB:
-                others.append(lambda: feat_regroup(i + 3))
-            if 0 <= i < NB:
-                others.append(lambda: quant_e(i, 0))
-                others.append(lambda: quant_e(i, 1))
-                others.append(lambda: recip(i))
-            weave(folds, others)
-            if folds:
-                bias(i + 3)
+            if 0 <= i < SEQS:
+                others.append(lambda: regroup_e(i, 0))
+                others.append(lambda: regroup_e(i, 1))
+            if 0 <= i + 1 < SEQS:
+                others.append(lambda: quantise_feature(i + 1))
+            if SCALAR_REGROUPS <= i + 3 < SEQS:
+                others.append(lambda: regroup_feature(i + 3))
+            if 0 <= i < SEQS:
+                others.append(lambda: quantise_e(i, 0))
+                others.append(lambda: quantise_e(i, 1))
+                others.append(lambda: invert_row_sums(i))
+            weave(maxima, others)
+            if maxima:
+                bias_of_exp(i + 3)
             if i >= 1:
-                finish(i - 1)
+                divide_and_store(i - 1)

from contextlib import ExitStack

import concourse.mybir as mybir
from concourse.masks import make_identity

FLOPS = 2 * 16 * 512 * 512 * 512

BF16 = mybir.dt.bfloat16
F32 = mybir.dt.float32
U32 = mybir.dt.uint32
U8 = mybir.dt.uint8
FP8X4 = mybir.dt.float8_e4m3fn_x4
ALU = mybir.AluOpType
ACT = mybir.ActivationFunctionType
AX = mybir.AxisListType

P = 128
SEQS = 16
Q = 4
W = 512
EPS = 1e-6
STATS = 6

SCALAR_VARIANCE_EVERY = 4
GPSIMD_REGROUPS = 10
SCALAR_REGROUPS = 15


def weave(first, second):
    for n in range(max(len(first), len(second))):
        for steps in (first, second):
            if n < len(steps):
                steps[n]()


def tile_frameaugment_t_kernel(tc, feature, noise, out):
    nc = tc.nc
    feature_quarters = feature.rearrange("b (t p) f -> b p t f", p=P)
    noise_quarters = noise.rearrange("b (t p) j -> b p t j", p=P)
    out_quarters = out.rearrange("b (t p) f -> b p t f", p=P)

    scalar_seqs = [b for b in range(SEQS) if b % SCALAR_VARIANCE_EVERY == 1]
    vector_seqs = [b for b in range(SEQS) if b % SCALAR_VARIANCE_EVERY != 1]
    col = dict((b, Q * n) for n, b in enumerate(vector_seqs + scalar_seqs))
    n_vector = Q * len(vector_seqs)
    n_scalar = Q * len(scalar_seqs)

    with ExitStack() as ctx:
        ctx.enter_context(tc.manual_schedule())
        keep = ctx.enter_context(tc.tile_pool(name="keep", bufs=1))
        inputs = ctx.enter_context(tc.tile_pool(name="inputs", bufs=SEQS + SEQS - SCALAR_REGROUPS))
        work = ctx.enter_context(tc.tile_pool(name="work", bufs=2))
        transposed_banks = ctx.enter_context(tc.psum_pool(name="transposed_banks", bufs=4))
        product_banks = ctx.enter_context(tc.psum_pool(name="product_banks", bufs=Q))

        feature_in = []
        for b in range(SEQS):
            tile_in = inputs.tile([P, Q, W], BF16, name="feature_in%d" % b, tag="inputs")
            if b < 2:
                for t in range(Q):
                    nc.sync.dma_start(out=tile_in[:, t, :], in_=feature_quarters[b][:, t, :])
            else:
                nc.sync.dma_start(out=tile_in[:], in_=feature_quarters[b])
            feature_in.append(tile_in)
        noise_in = []
        for b in range(SEQS):
            tile_in = inputs.tile([P, Q, W], BF16, name="noise_in%d" % b, tag="inputs")
            nc.sync.dma_start(out=tile_in[:], in_=noise_quarters[b])
            noise_in.append(tile_in)

        zero = keep.tile([P, 1], F32)
        nc.vector.memset(zero[:], 0.0)
        one = keep.tile([P, 1], F32)
        nc.scalar.activation(out=one[:], in_=zero[:], func=ACT.Exp)
        identity_bf16 = keep.tile([P, P], BF16)
        make_identity(nc, identity_bf16[:])
        identity_f32 = keep.tile([P, P], F32)
        make_identity(nc, identity_f32[:])

        stats = keep.tile([P, n_vector, STATS], F32)
        sums = keep.tile([P, n_scalar], F32)
        neg_means = keep.tile([P, n_scalar], F32)
        scalar_m2 = keep.tile([P, n_scalar], F32)
        mean_gap = keep.tile([P, n_vector], F32)
        gap_term = keep.tile([P, n_vector], F32)
        m2_even_odd = keep.tile([P, n_vector], F32)
        spread = keep.tile([P, SEQS * Q], F32)
        inv_spread = keep.tile([P, SEQS * Q], F32)
        stability = keep.tile([P, SEQS * Q], F32)
        partition_min = keep.tile([P, 1], F32)
        global_min = keep.tile([P, 1], F32)
        row_max = [keep.tile([P, Q], F32, name="row_max%d" % b) for b in range(SEQS)]
        exp_bias = [keep.tile([P, Q], F32, name="exp_bias%d" % b) for b in range(SEQS)]
        row_sum = [keep.tile([P, Q], F32, name="row_sum%d" % b) for b in range(SEQS)]
        inv_row_sum = [keep.tile([P, Q], F32, name="inv_row_sum%d" % b) for b in range(SEQS)]
        feature_codes = [keep.tile([P, W], U32, name="feature_codes%d" % b, align_bytes=64) for b in range(SEQS)]
        feature_scales = [keep.tile([P, W], U8, name="feature_scales%d" % b, align_bytes=64) for b in range(SEQS)]

        feature_grouped = {}
        e_rows = {}
        e_transposed = {}
        e_grouped = {}
        e_quantised = {}
        products = {}


        def scalar_variance(b):
            first = col[b] - n_vector
            for t in range(Q):
                unused = work.tile([P, W], BF16, name="unused", tag="unused")
                nc.scalar.activation(out=unused[:], in_=feature_in[b][:, t, :], func=ACT.Copy,
                                     accum_out=sums[:, first + t:first + t + 1])
            nc.scalar.mul(out=neg_means[:, first:first + Q], in_=sums[:, first:first + Q], mul=-1.0 / W)
            for t in range(Q):
                unused = work.tile([P, W], BF16, name="unused", tag="unused")
                nc.scalar.activation(out=unused[:], in_=feature_in[b][:, t, :], func=ACT.Square,
                                     bias=neg_means[:, first + t:first + t + 1],
                                     accum_out=scalar_m2[:, first + t:first + t + 1])

        def regroup_feature(b):
            grouped = work.tile([P, W, Q], BF16, name="feature_grouped", tag="feature_grouped", align_bytes=64,
                                bufs=SCALAR_REGROUPS + 1)
            feature_grouped[b] = grouped
            grouped_by_fours = grouped[:].rearrange("p (c i) t -> p c t i", i=4)
            in_by_fours = feature_in[b][:].rearrange("p t (c i) -> p c t i", i=4)
            if b < GPSIMD_REGROUPS:
                nc.gpsimd.tensor_scalar(out=grouped[:], in0=feature_in[b][:].rearrange("p t f -> p f t"),
                                        scalar1=1.0, scalar2=0.0, op0=ALU.mult, op1=ALU.add)
            elif b < SCALAR_REGROUPS:
                nc.scalar.copy(out=grouped_by_fours, in_=in_by_fours)
            else:
                nc.vector.tensor_copy(out=grouped_by_fours, in_=in_by_fours)

        def quantise_feature(b):
            nc.vector.quantize_mx(out=feature_codes[b][:].bitcast(FP8X4), scales=feature_scales[b][:],
                                  in_=feature_grouped[b][:].rearrange("p f t -> p (f t)"))

        def row_max_steps(b):
            widths = (W // 2, W // 4, W // 8, W // 16)
            folded = [work.tile([P, Q, w], BF16, name="folded%d" % w, tag="folded%d" % w) for w in widths]
            sources = [noise_in[b]] + folded[:-1]

            def fold(n):
                w = widths[n]
                return lambda: nc.vector.tensor_tensor(out=folded[n][:], in0=sources[n][:, :, 0:w],
                                                       in1=sources[n][:, :, w:2 * w], op=ALU.max)

            steps = [fold(n) for n in range(len(widths))]
            steps.append(lambda: nc.vector.tensor_reduce(out=row_max[b][:], in_=folded[-1][:], axis=AX.X, op=ALU.max))
            return steps

        def bias_of_exp(b):
            nc.vector.scalar_tensor_tensor(out=exp_bias[b][:], in0=stability[:, col[b]:col[b] + Q], scalar=-1.0,
                                           in1=row_max[b][:], op0=ALU.mult, op1=ALU.mult)

        def exponentials(b):
            e_rows[b] = work.tile([P, Q, W], BF16, name="e_rows", tag="e_rows")
            for t in range(Q):
                nc.scalar.activation(out=e_rows[b][:, t, :], in_=noise_in[b][:, t, :], func=ACT.Exp,
                                     bias=exp_bias[b][:, t:t + 1], scale=stability[:, col[b] + t:col[b] + t + 1],
                                     accum_out=row_sum[b][:, t:t + 1])

        def transposes(b):
            e_transposed[b] = []
            for half in range(2):
                bank = transposed_banks.tile([P, 2, Q, P], BF16, name="e_transposed", tag="e_transposed")
                for u in range(2):
                    for k in range(Q):
                        nc.tensor.transpose(bank[:, u, k, :], e_rows[b][:, 2 * half + u, P * k:P * k + P],
                                            identity_bf16[:])
                e_transposed[b].append(bank)

        def regroup_e(b, half):
            if half == 0:
                e_grouped[b] = work.tile([P, Q, P, Q], BF16, name="e_grouped", tag="e_grouped", align_bytes=64)
            nc.vector.tensor_copy(out=e_grouped[b][:, 2 * half:2 * half + 2, :, :],
                                  in_=e_transposed[b][half][:].rearrange("p u k i -> p u i k"))

        def quantise_e(b, half):
            if half == 0:
                e_quantised[b] = (work.tile([P, W], U32, name="e_codes", tag="e_codes", align_bytes=64),
                                  work.tile([P, W], U8, name="e_scales", tag="e_scales", align_bytes=64))
            codes, scales = e_quantised[b]
            cols = slice(2 * P * half, 2 * P * (half + 1))
            nc.vector.quantize_mx(out=codes[:, cols].bitcast(FP8X4), scales=scales[:, cols],
                                  in_=e_grouped[b][:, 2 * half:2 * half + 2, :, :].rearrange("p u i k -> p (u i k)"))

        def invert_row_sums(b):
            nc.vector.reciprocal(out=inv_row_sum[b][:], in_=row_sum[b][:])

        def multiply(b):
            codes, scales = e_quantised[b]
            products[b] = []
            for t in range(Q):
                bank = product_banks.tile([P, W], F32, name="product", tag="product")
                nc.tensor.matmul_mx(out=bank[:], lhsT=codes[:, P * t:P * t + P].bitcast(FP8X4),
                                    lhsT_scale=scales[:, P * t:P * t + P],
                                    rhs=feature_codes[b][:].bitcast(FP8X4), rhs_scale=feature_scales[b][:],
                                    start=True, stop=True)
                products[b].append(bank)

        def divide_and_store(b):
            last = b == SEQS - 1
            result = work.tile([P, Q, W], F32, name="result", tag="result", bufs=3)
            for t in range(Q):
                if last and t % 2 == 1:
                    nc.vector.tensor_scalar(out=result[:, t, :], in0=products[b][t][:],
                                            scalar1=inv_row_sum[b][:, t:t + 1], scalar2=None, op0=ALU.mult)
                    nc.sync.dma_start(out=out_quarters[b][:, t - 1:t + 1, :], in_=result[:, t - 1:t + 1, :])
                else:
                    nc.scalar.activation(out=result[:, t, :], in_=products[b][t][:], func=ACT.Copy,
                                         scale=inv_row_sum[b][:, t:t + 1])
            if not last:
                nc.sync.dma_start(out=out_quarters[b], in_=result[:])

        for b in scalar_seqs:
            scalar_variance(b)
        for b in range(SCALAR_REGROUPS):
            regroup_feature(b)
        for b in vector_seqs:
            for t in range(Q):
                nc.vector.bn_stats(out=stats[:, col[b] + t, :], in_=feature_in[b][:, t, :])

        all_minima = product_banks.tile([P, P], F32, name="all_minima", tag="product")
        chain = [
            lambda: nc.vector.tensor_tensor(out=mean_gap[:], in0=stats[:, :, 1], in1=stats[:, :, 4], op=ALU.subtract),
            lambda: nc.vector.scalar_tensor_tensor(out=m2_even_odd[:], in0=stats[:, :, 2], scalar=EPS * (W - 1),
                                                   in1=stats[:, :, 5], op0=ALU.add, op1=ALU.add),
            lambda: nc.vector.scalar_tensor_tensor(out=gap_term[:], in0=mean_gap[:], scalar=float(W // 4),
                                                   in1=mean_gap[:], op0=ALU.mult, op1=ALU.mult),
            lambda: nc.vector.tensor_scalar(out=spread[:, n_vector:], in0=scalar_m2[:], scalar1=EPS * (W - 1),
                                            scalar2=None, op0=ALU.add),
            lambda: nc.vector.tensor_tensor(out=spread[:, 0:n_vector], in0=gap_term[:], in1=m2_even_odd[:], op=ALU.add),
            lambda: nc.vector.tensor_reduce(out=partition_min[:], in_=spread[:], axis=AX.X, op=ALU.min),
            lambda: nc.tensor.transpose(all_minima[:], partition_min[:].to_broadcast([P, P]), identity_f32[:]),
            lambda: nc.vector.reciprocal(out=inv_spread[:], in_=spread[:]),
            lambda: nc.vector.tensor_reduce(out=global_min[:], in_=all_minima[:], axis=AX.X, op=ALU.min),
            lambda: nc.vector.tensor_scalar(out=stability[:], in0=inv_spread[:], scalar1=global_min[:, 0:1],
                                            scalar2=None, op0=ALU.mult),
            lambda: bias_of_exp(0),
        ]
        weave(chain, [step for pair in zip(row_max_steps(0), row_max_steps(1)) for step in pair])
        bias_of_exp(1)

        for i in range(-2, SEQS + 1):
            if i + 2 < SEQS:
                exponentials(i + 2)
            if 0 <= i + 1 < SEQS:
                transposes(i + 1)
            if i >= 1:
                multiply(i - 1)
            maxima = row_max_steps(i + 3) if 2 <= i + 3 < SEQS else []
            others = []
            if 0 <= i < SEQS:
                others.append(lambda: regroup_e(i, 0))
                others.append(lambda: regroup_e(i, 1))
            if 0 <= i + 1 < SEQS:
                others.append(lambda: quantise_feature(i + 1))
            if SCALAR_REGROUPS <= i + 3 < SEQS:
                others.append(lambda: regroup_feature(i + 3))
            if 0 <= i < SEQS:
                others.append(lambda: quantise_e(i, 0))
                others.append(lambda: quantise_e(i, 1))
                others.append(lambda: invert_row_sums(i))
            weave(maxima, others)
            if maxima:
                bias_of_exp(i + 3)
            if i >= 1:
                divide_and_store(i - 1)
